import numpy as np
import ml_dtypes


def mxq(x, axis, fmt="e4m3"):
    dtype, down = {"e4m3": (ml_dtypes.float8_e4m3fn, 7), "e5m2": (ml_dtypes.float8_e5m2, 14)}[fmt]
    v = np.moveaxis(np.asarray(x, np.float32).astype(ml_dtypes.bfloat16).astype(np.float64), axis, -1)
    blocks = v.reshape(v.shape[:-1] + (-1, 32))
    amax = np.abs(blocks).max(-1, keepdims=True)
    byte = np.maximum(np.where(amax > 0, np.frexp(amax)[1] - 1 + 127, 0) - down, 1)
    scale = np.exp2(byte - 127.0)
    codes = (blocks / scale).astype(np.float32).astype(dtype).astype(np.float64)
    return np.moveaxis((codes * scale).reshape(v.shape), -1, axis)


WIDE = False


def mx_kscale(k):
    if not WIDE:
        return np.ones(k)
    levels = np.array([10, -10, 5, -5, 0])
    if k % 512:
        return np.exp2(np.random.permutation(np.resize(levels, k // 32))).repeat(32)
    a = np.empty((k // 512, 16))
    for p in range(k // 512):
        a[p, :8] = np.random.permutation(np.resize(levels, 8))
        for g in range(8):
            far = levels[np.abs(levels - a[p, g]) >= 10]
            a[p, g + 8] = far[np.random.randint(len(far))]
    return np.exp2(a.ravel()).repeat(32)


BF16 = ml_dtypes.bfloat16


def bf(x):
    return np.asarray(x, np.float32).astype(BF16)


def f64(x):
    return np.asarray(x).astype(np.float64)


B, S, D, H, DH, DV, R = 4, 256, 2048, 16, 128, 128, 512
EPS = 1e-6
ROPE_THETA = 10000.0


def rms_norm(c, w):
    var = np.mean(np.square(c), axis=-1, keepdims=True)
    return c * (1.0 / np.sqrt(var + EPS)) * w


def apply_rope(t, cos, sin):
    b, s, h, d = t.shape
    tr = t.reshape(b, s, h, d // 2, 2)
    x1, x2 = tr[..., 0], tr[..., 1]
    c = cos[None, :, None, :]
    sn = sin[None, :, None, :]
    o1 = x1 * c - x2 * sn
    o2 = x1 * sn + x2 * c
    return np.stack([o1, o2], axis=-1).reshape(b, s, h, d)


def draw0():
    s = mx_kscale(D)
    t = mx_kscale(R)
    inv_freq = 1.0 / ROPE_THETA ** (np.arange(0, DH, 2) / DH)
    ang = np.arange(S)[:, None] * inv_freq[None, :]
    return {"x": bf(np.random.standard_normal((B, S, D)) * s),
            "freqs_cos": bf(np.cos(ang)),
            "freqs_sin": bf(np.sin(ang)),
            "w_kv_compress": bf(np.random.standard_normal((D, R)) / np.sqrt(D) / s[:, None]),
            "kv_norm_w": bf((1.0 + 0.1 * np.random.standard_normal(R)) * t),
            "w_k_up": bf(np.random.standard_normal((R, H * DH)) / np.sqrt(R) / t[:, None]),
            "w_v_up": bf(np.random.standard_normal((R, H * DV)) / np.sqrt(R) / t[:, None])}


def core(x, freqs_cos, freqs_sin, w_kv_compress, kv_norm_w, w_k_up, w_v_up):
    c = mxq(f64(x), 2, "e4m3") @ mxq(f64(w_kv_compress), 0, "e4m3")
    latent_q = mxq(rms_norm(c, f64(kv_norm_w)), 2, "e4m3")
    k = (latent_q @ mxq(f64(w_k_up), 0, "e4m3")).reshape(B, S, H, DH)
    v = (latent_q @ mxq(f64(w_v_up), 0, "e4m3")).reshape(B, S, H, DV)
    return apply_rope(k, f64(freqs_cos), f64(freqs_sin)), v


def e4m3fn_bytes(y):
    return np.clip(np.asarray(y, np.float64), -448.0, 448.0).astype(np.float32).astype(ml_dtypes.float8_e4m3fn).view(np.uint8)


def e4m3fn_values(b):
    return np.asarray(b, np.uint8).view(ml_dtypes.float8_e4m3fn).astype(np.float64)


def setup_inputs():
    d = draw0()
    x0 = np.asarray(d['x']).astype(np.float64)
    s = (np.max(np.abs(x0), axis=(0, 1), keepdims=True) / 448.0).astype(np.float32)
    out = {}
    for k, v in d.items():
        if k == 'x':
            out['x_bytes'] = e4m3fn_bytes(x0 / s.astype(np.float64))
            out['x_scale'] = s
        else:
            out[k] = v
    return out


def reference(x_bytes, x_scale, freqs_cos, freqs_sin, w_kv_compress, kv_norm_w, w_k_up, w_v_up):
    return core(e4m3fn_values(x_bytes) * x_scale.astype(np.float64), freqs_cos, freqs_sin, w_kv_compress, kv_norm_w, w_k_up, w_v_up)

@@ -1,0 +1,417 @@
+from contextlib import ExitStack
+
+import concourse.mybir as mybir
+from concourse.masks import make_identity
+
+B, S, D, H, DH, R = 4, 256, 2048, 16, 128, 512
+HALF = DH // 2
+FLOPS = 2 * B * S * R * (D + 2 * H * DH)
+
+F32 = mybir.dt.float32
+BF16 = mybir.dt.bfloat16
+U32 = mybir.dt.uint32
+U8 = mybir.dt.uint8
+FP8 = mybir.dt.float8_e4m3fn
+FP8X4 = mybir.dt.float8_e4m3fn_x4
+MULT = mybir.AluOpType.mult
+ADD = mybir.AluOpType.add
+SUB = mybir.AluOpType.subtract
+ACT = mybir.ActivationFunctionType
+
+P = 128
+GROUPS = D // 512
+BANKS = {"a": 2, "b": 1, "c": 1, "v": 2, "tr": 2}
+EPS = 1e-6
+
+
+def tile_mla_pa_kernel(tc, x_bytes, x_scale, freqs_cos, freqs_sin, w_kv_compress, kv_norm_w, w_k_up, w_v_up, out_0, out_1):
+    nc = tc.nc
+    with ExitStack() as ctx:
+        keep = ctx.enter_context(tc.tile_pool(name="keep", bufs=1))
+        ld = ctx.enter_context(tc.tile_pool(name="ld", bufs=1))
+        wk = ctx.enter_context(tc.tile_pool(name="wk", bufs=1))
+        ps = ctx.enter_context(tc.psum_pool(name="ps", bufs=1))
+
+        ctx.enter_context(tc.manual_schedule())
+        xb = {}
+
+        def load_x(q, m):
+            xb[q, m] = ld.tile([P, D], U8, name=f"xb{q}_{m}", tag="xb", bufs=8)
+            nc.sync.dma_start(out=xb[q, m][:], in_=x_bytes[q, m * P : (m + 1) * P, :])
+
+        wc_raw = {}
+
+        def load_wc(g):
+            wc_raw[g] = ld.tile([P, 4, R], BF16, name=f"wcr{g}", tag="wcr", bufs=4)
+            nc.sync.dma_start(out=wc_raw[g][:], in_=w_kv_compress[g * 512 : (g + 1) * 512, :].rearrange("(p t) n -> p t n", t=4))
+
+        wu_raw = {}
+
+        def load_wu(kind, w, c):
+            wu_raw[kind, c] = ld.tile([P, 4, 1024], BF16, name=f"wr{kind}{c}", tag="wr", bufs=4)
+            nc.sync.dma_start(out=wu_raw[kind, c][:], in_=w.rearrange("(p t) n -> p t n", t=4)[:, :, c * 1024 : (c + 1) * 1024])
+
+        scale = keep.tile([P, GROUPS, 4], F32, name="scale")
+        cos = keep.tile([P, 2, HALF], BF16, name="cos")
+        sin = keep.tile([P, 2, HALF], BF16, name="sin")
+        nw = keep.tile([P, R], BF16, name="nw")
+        load_x(0, 0)
+        load_wc(0)
+        load_x(0, 1)
+        for g in range(1, GROUPS):
+            load_wc(g)
+        load_x(1, 0)
+        load_x(1, 1)
+        load_wu("k", w_k_up, 0)
+        load_wu("k", w_k_up, 1)
+        load_wu("v", w_v_up, 0)
+        load_x(2, 0)
+        load_x(2, 1)
+        load_wu("v", w_v_up, 1)
+        load_x(3, 0)
+        load_x(3, 1)
+        nc.scalar.dma_start(out=scale[:], in_=x_scale.rearrange("a b (g p t) -> p (a b g) t", p=P, t=4))
+        nc.scalar.dma_start(out=nw[:], in_=kv_norm_w.partition_broadcast(P))
+        nc.scalar.dma_start(out=cos[:], in_=freqs_cos.rearrange("(s p) i -> p s i", p=P))
+        nc.scalar.dma_start(out=sin[:], in_=freqs_sin.rearrange("(s p) i -> p s i", p=P))
+        warm = keep.tile([P, 1], F32, name="warm")
+        nc.vector.memset(warm[:], 1.0)
+        warm_out = keep.tile([P, 1], F32, name="warm_out")
+        nc.scalar.activation(out=warm_out[:], in_=warm[:], func=ACT.Sqrt)
+        ident = keep.tile([P, P], F32, name="ident")
+        make_identity(nc, ident[:])
+        ident_bf = keep.tile([P, P], BF16, name="ident_bf")
+        nc.vector.tensor_copy(out=ident_bf[:], in_=ident[:])
+
+        rot = keep.tile([P, 2, HALF, 2], F32, name="rot")
+        gain = keep.tile([P, R], BF16, name="gain")
+
+        def lay(eng, out, in_):
+            if eng == "v":
+                nc.vector.tensor_copy(out=out, in_=in_)
+            elif eng == "g":
+                nc.gpsimd.tensor_scalar(out=out, in0=in_, scalar1=1.0, scalar2=0.0, op0=MULT, op1=ADD)
+            else:
+                nc.scalar.copy(out=out, in_=in_)
+
+        codes = {}
+        scales = {}
+        for kind, width in (("c", GROUPS * R), ("k", H * DH), ("v", H * DH)):
+            codes[kind] = keep.tile([P, width], U32, name=f"codes_{kind}", align_bytes=64)
+            scales[kind] = keep.tile([P, width], U8, name=f"scales_{kind}", align_bytes=64)
+
+        def quant(cd, sc, lo, width, grouped):
+            nc.vector.quantize_mx(out=cd[:, lo : lo + width].bitcast(FP8X4), scales=sc[:, lo : lo + width], in_=grouped)
+
+        wg = {}
+
+        def w_lay(kind, c, j, eng):
+            if (kind, c) not in wg:
+                wg[kind, c] = wk.tile([P, 512, 4], BF16, name=f"wg_{kind}{c}", tag="wg", bufs=5, align_bytes=64)
+            out = wg[kind, c][:, j * 256 : (j + 1) * 256, :]
+            if kind == "c":
+                lay(eng, out.rearrange("q (p e) t -> q p e t", e=2), wc_raw[c][:].rearrange("q t (p u e) -> q u p e t", u=2, e=2)[:, j])
+            elif kind == "k":
+                lay(eng, out, wu_raw["k", c // 2][:, :, (c % 2) * 512 : (c % 2 + 1) * 512].rearrange("p t (n j) -> p j n t", j=2)[:, 1 - j])
+            else:
+                lo = (c % 2) * 512 + j * 256
+                lay(eng, out, wu_raw["v", c // 2][:, :, lo : lo + 256].rearrange("p t n -> p n t"))
+
+        def w_turn(kind, c, j, tag, eng):
+            if (kind, c) not in wg:
+                wg[kind, c] = wk.tile([P, 512, 4], BF16, name=f"wg_{kind}{c}", tag="wg", bufs=5, align_bytes=64)
+            if kind == "c":
+                src = wc_raw[c][:].rearrange("q t (p u e) -> q u p e t", u=2, e=2)[:, j]
+            else:
+                src = wu_raw["k", c // 2][:, :, (c % 2) * 512 : (c % 2 + 1) * 512].rearrange("p t (n j) -> p j n t", j=2)[:, 1 - j]
+            bank = ps.tile([P, 1024], BF16, name=f"wt_{kind}{c}_{j}", tag=tag, bufs=BANKS[tag])
+            for h in range(2):
+                if kind == "c":
+                    nc.tensor.matmul(bank[:, h * 512 : (h + 1) * 512].rearrange("q (p e t) -> q p e t", e=2, t=4), lhsT=ident_bf[:], rhs=src[:, h * 64 : (h + 1) * 64], start=True, stop=True)
+                else:
+                    nc.tensor.matmul(bank[:, h * 512 : (h + 1) * 512].rearrange("p (n t) -> p n t", t=4), lhsT=ident_bf[:], rhs=src[:, h * P : (h + 1) * P], start=True, stop=True)
+            out = wg[kind, c][:, j * 256 : (j + 1) * 256, :].rearrange("p n t -> p (n t)")
+            if eng == "v":
+                nc.vector.tensor_copy(out=out, in_=bank[:])
+            else:
+                nc.scalar.copy(out=out, in_=bank[:])
+
+        def w_quant(kind, c):
+            quant(codes[kind], scales[kind], c * 512, 512, wg[kind, c][:].rearrange("p n t -> p (n t)"))
+
+        xs = {}
+        xg = {}
+        x_codes = {}
+        x_scales = {}
+
+        def cast(q, k, eng):
+            m, h = k % 2, k // 2
+            if k < 2:
+                xs[q, m] = wk.tile([P, D], BF16, name=f"xs{q}_{m}", tag="xs", bufs=4)
+            out = xs[q, m][:, h * 1024 : (h + 1) * 1024]
+            in_ = xb[q, m][:, h * 1024 : (h + 1) * 1024].bitcast(FP8)
+            if eng == "v":
+                nc.vector.tensor_copy(out=out, in_=in_)
+            else:
+                nc.scalar.copy(out=out, in_=in_)
+
+        trs = {}
+
+        def turn(q, g):
+            tr = ps.tile([P, 2, 256], F32, name=f"tr{q}_{g}", tag="tr", bufs=2)
+            trs[q, g] = tr
+            for m in range(2):
+                words = xs[q, m][:].bitcast(F32)
+                for u in range(2):
+                    nc.tensor.transpose(tr[:, u, m * P : (m + 1) * P], words[:, 256 * g + u : 256 * (g + 1) : 2], ident[:])
+
+        def prod(q, g):
+            if g == 0:
+                xg[q] = wk.tile([P, GROUPS, 256, 4], BF16, name=f"xg{q}", tag="xg", bufs=2, align_bytes=64)
+                x_codes[q] = wk.tile([P, GROUPS * 256], U32, name=f"xc{q}", tag="xc", bufs=2, align_bytes=64)
+                x_scales[q] = wk.tile([P, GROUPS * 256], U8, name=f"xq{q}", tag="xq", bufs=2, align_bytes=64)
+            nc.vector.tensor_tensor(
+                out=xg[q][:, g].rearrange("p r (u e) -> p r u e", e=2),
+                in0=trs[q, g][:].bitcast(BF16).rearrange("p u (r e) -> p r u e", e=2),
+                in1=scale[:, g, :].rearrange("p (u e) -> p u e", e=2).unsqueeze(1).to_broadcast([P, 256, 2, 2]),
+                op=MULT)
+
+        def x_quant(q, i):
+            quant(x_codes[q], x_scales[q], i * 512, 512, xg[q][:, 2 * i : 2 * i + 2].rearrange("p g r t -> p (g r t)"))
+
+        cs = {}
+        sds = {}
+        lat = {}
+        l_codes = {}
+        l_scales = {}
+        lts = {}
+        lgs = {}
+
+        def compress(q, m):
+            tag = "c" if m == 0 or q in (1, 2) else "v" if q == 0 else "tr"
+            c = ps.tile([P, R], F32, name=f"c{q}_{m}", tag=tag, bufs=1 if tag == "c" else 2)
+            cs[q, m] = c
+            for g in range(GROUPS):
+                lo = g * 256 + m * P
+                nc.tensor.matmul_mx(
+                    out=c[:], lhsT=x_codes[q][:, lo : lo + P].bitcast(FP8X4), lhsT_scale=x_scales[q][:, lo : lo + P],
+                    rhs=codes["c"][:, g * R : (g + 1) * R].bitcast(FP8X4), rhs_scale=scales["c"][:, g * R : (g + 1) * R],
+                    start=(g == 0), stop=(g == GROUPS - 1))
+
+        def rms(q, m):
+            junk = wk.tile([P, R], BF16, name=f"junk{q}_{m}", tag="junk", bufs=2)
+            ss = wk.tile([P, 1], F32, name=f"ss{q}_{m}", tag="ss", bufs=4)
+            nc.scalar.activation(out=junk[:], in_=cs[q, m][:], func=ACT.Square, accum_out=ss[:])
+            sds[q, m] = wk.tile([P, 1], F32, name=f"sd{q}_{m}", tag="sd", bufs=4)
+            nc.scalar.activation(out=sds[q, m][:], in_=ss[:], func=ACT.Sqrt, bias=EPS, scale=1.0 / R)
+
+        def norm(q, m):
+            rs = wk.tile([P, 1], F32, name=f"rs{q}_{m}", tag="rs", bufs=4)
+            nc.vector.reciprocal(rs[:], sds[q, m][:])
+            lat[q, m] = wk.tile([P, R], BF16, name=f"lat{q}_{m}", tag="lat", bufs=4)
+            nc.vector.scalar_tensor_tensor(out=lat[q, m][:], in0=cs[q, m][:], scalar=rs[:], in1=gain[:], op0=MULT, op1=MULT)
+
+        def l_turn(q):
+            lts[q] = ps.tile([P, 2, 256], F32, name=f"lt{q}", tag="tr", bufs=2)
+            for m in range(2):
+                words = lat[q, m][:].bitcast(F32)
+                for u in range(2):
+                    nc.tensor.transpose(lts[q][:, u, m * P : (m + 1) * P], words[:, u * P : (u + 1) * P], ident[:])
+
+        def l_lay(q):
+            lgs[q] = wk.tile([P, 256, 4], BF16, name=f"lg{q}", tag="lg", bufs=2, align_bytes=64)
+            nc.scalar.copy(out=lgs[q][:].rearrange("p r t -> p (r t)").bitcast(F32).rearrange("p (r u) -> p r u", u=2), in_=lts[q][:].rearrange("p u r -> p r u"))
+
+        def l_quant(q):
+            l_codes[q] = wk.tile([P, 256], U32, name=f"lc{q}", tag="lc", bufs=4, align_bytes=64)
+            l_scales[q] = wk.tile([P, 256], U8, name=f"lq{q}", tag="lq", bufs=4, align_bytes=64)
+            quant(l_codes[q], l_scales[q], 0, 256, lgs[q][:].rearrange("p r t -> p (r t)"))
+
+        def up(q, m, kind, lo, width, out, start, stop):
+            nc.tensor.matmul_mx(
+                out=out, lhsT=l_codes[q][:, m * P : (m + 1) * P].bitcast(FP8X4), lhsT_scale=l_scales[q][:, m * P : (m + 1) * P],
+                rhs=codes[kind][:, lo : lo + width].bitcast(FP8X4), rhs_scale=scales[kind][:, lo : lo + width], start=start, stop=stop)
+
+        bs = {}
+        az = {}
+
+        def k_b(s):
+            q, m, half = s // 4, s // 2 % 2, s % 2
+            bs[s] = ps.tile([P, 512], F32, name=f"b{s}", tag="b", bufs=1)
+            for hh in range(2):
+                lo = (2 * half + hh) * 512
+                up(q, m, "k", lo, 256, bs[s][:, hh * 256 : (hh + 1) * 256], True, False)
+                up(q, m, "k", lo + 256, 256, bs[s][:, hh * 256 : (hh + 1) * 256], False, True)
+
+        def k_a(s):
+            q, m, half = s // 4, s // 2 % 2, s % 2
+            for hh in range(2):
+                az[s, hh] = ps.tile([P, 512], F32, name=f"a{s}_{hh}", tag="a", bufs=2)
+                up(q, m, "k", (2 * half + hh) * 512, 512, az[s, hh][:], True, True)
+
+        pts = {}
+        qts = {}
+
+        def k_p(s):
+            m = s // 2 % 2
+            pts[s] = wk.tile([P, 512], F32, name=f"pt{s}", tag="pt", bufs=3)
+            nc.vector.tensor_tensor(
+                out=pts[s][:].rearrange("p (h i) -> p h i", i=HALF), in0=bs[s][:].rearrange("p (h i) -> p h i", i=HALF),
+                in1=cos[:, m, :].unsqueeze(1).to_broadcast([P, 8, HALF]), op=MULT)
+
+        def k_q(s, hh):
+            m = s // 2 % 2
+            qts[s, hh] = wk.tile([P, 512], F32, name=f"qt{s}_{hh}", tag="qt", bufs=5)
+            nc.vector.tensor_tensor(
+                out=qts[s, hh][:].rearrange("p (h i j) -> p h i j", i=HALF, j=2),
+                in0=az[s, hh][:].rearrange("p (j h i) -> p h i j", j=2, i=HALF),
+                in1=rot[:, m].unsqueeze(1).to_broadcast([P, 4, HALF, 2]), op=MULT)
+
+        oks = {}
+
+        def k_add(s, hh, eng):
+            if hh == 0:
+                oks[s] = wk.tile([P, 1024], F32, name=f"ok{s}", tag="ok", bufs=4)
+            e = nc.gpsimd if eng == "g" else nc.vector
+            e.tensor_tensor(
+                out=oks[s][:, hh * 512 : (hh + 1) * 512].rearrange("p (n j) -> p n j", j=2),
+                in0=pts[s][:, hh * 256 : (hh + 1) * 256].unsqueeze(2).to_broadcast([P, 256, 2]),
+                in1=qts[s, hh][:].rearrange("p (n j) -> p n j", j=2), op=ADD)
+
+        def k_store(s):
+            q, m, half = s // 4, s // 2 % 2, s % 2
+            nc.sync.dma_start(out=out_0[q, m * P : (m + 1) * P].rearrange("s h d -> s (h d)")[:, half * 1024 : (half + 1) * 1024], in_=oks[s][:])
+
+        vs = {}
+
+        def v_mm(s):
+            q, m, half = s // 4, s // 2 % 2, s % 2
+            for hh in range(2):
+                vs[s, hh] = ps.tile([P, 512], F32, name=f"v{s}_{hh}", tag="v", bufs=2)
+                up(q, m, "v", (2 * half + hh) * 512, 512, vs[s, hh][:], True, True)
+
+        def v_out(s):
+            q, m, half = s // 4, s // 2 % 2, s % 2
+            ov = wk.tile([P, 1024], F32, name=f"ov{s}", tag="ov", bufs=4)
+            for hh in range(2):
+                nc.scalar.copy(out=ov[:, hh * 512 : (hh + 1) * 512], in_=vs[s, hh][:])
+            nc.sync.dma_start(out=out_1[q, m * P : (m + 1) * P].rearrange("s h d -> s (h d)")[:, half * 1024 : (half + 1) * 1024], in_=ov[:])
+
+        cast(0, 0, "s")
+        cast(0, 2, "s")
+        cast(0, 1, "v")
+        cast(0, 3, "v")
+        w_turn("c", 0, 0, "v", "s")
+        w_turn("c", 0, 1, "v", "s")
+        turn(0, 0)
+        turn(0, 1)
+        prod(0, 0)
+        w_turn("c", 1, 0, "a", "s")
+        w_turn("c", 1, 1, "a", "s")
+        turn(0, 2)
+        prod(0, 1)
+        w_quant("c", 0)
+        turn(0, 3)
+        w_turn("c", 2, 0, "v", "s")
+        w_turn("c", 2, 1, "v", "s")
+        prod(0, 2)
+        x_quant(0, 0)
+        w_quant("c", 1)
+        cast(1, 0, "s")
+        cast(1, 1, "s")
+        prod(0, 3)
+        w_turn("c", 3, 0, "a", "s")
+        w_turn("c", 3, 1, "a", "s")
+        w_quant("c", 2)
+        x_quant(0, 1)
+        turn(1, 0)
+        w_quant("c", 3)
+        nc.vector.scalar_tensor_tensor(out=rot[:, :, :, 0], in0=cos[:], scalar=-1.0, in1=sin[:], op0=MULT, op1=SUB)
+        nc.vector.scalar_tensor_tensor(out=rot[:, :, :, 1], in0=cos[:], scalar=-1.0, in1=sin[:], op0=MULT, op1=ADD)
+        nc.vector.tensor_copy(out=gain[:].rearrange("q (u p e) -> q u p e", u=2, e=2), in_=nw[:].rearrange("q (p u e) -> q u p e", u=2, e=2))
+        compress(0, 0)
+        compress(0, 1)
+        rms(0, 0)
+        rms(0, 1)
+        cast(1, 2, "s")
+        cast(1, 3, "s")
+        w_turn("k", 0, 0, "a", "s")
+        w_turn("k", 0, 1, "a", "s")
+        prod(1, 0)
+        turn(1, 1)
+        turn(1, 2)
+        norm(0, 0)
+        norm(0, 1)
+        l_turn(0)
+        l_lay(0)
+        w_turn("k", 1, 0, "a", "s")
+        w_turn("k", 1, 1, "a", "s")
+        w_turn("k", 2, 0, "a", "s")
+        w_turn("k", 2, 1, "a", "s")
+        prod(1, 1)
+        w_quant("k", 0)
+        prod(1, 2)
+        l_quant(0)
+        w_quant("k", 1)
+        k_b(0)
+        x_quant(1, 0)
+        w_quant("k", 2)
+        w_turn("k", 3, 0, "a", "s")
+        w_turn("k", 3, 1, "a", "s")
+        cast(2, 0, "s")
+        k_a(0)
+
+        extra_lay = {0: [("v", 0, 0, "s")], 1: [("v", 0, 1, "s"), ("v", 1, 0, "s")], 2: [("v", 1, 1, "s"), ("v", 2, 0, "s")], 3: [("v", 2, 1, "s"), ("v", 3, 0, "s")], 4: [("v", 3, 1, "s")]}
+        extra_quant = {0: [("k", 3)], 2: [("v", 0)], 3: [("v", 1)], 4: [("v", 2)], 5: [("v", 3)]}
+        v_done = 0
+        LEAD = 7
+        for s in range(16):
+            q, i = s // 4, s % 4
+            nxt = q + 1 < B
+            n = s + LEAD
+            c = s + LEAD + 2
+            if c < 16:
+                cast(c // 4, c % 4, "s")
+            if nxt and i >= 2 and (q < 2 or i == 3):
+                norm(q + 1, i - 2)
+            if nxt and i == 3:
+                l_turn(q + 1)
+                l_lay(q + 1)
+            if n < 16:
+                turn(n // 4, n % 4)
+            k_p(s)
+            pend = n - 1
+            if pend < 16 and pend % 2 == 1:
+                x_quant(pend // 4, pend % 4 // 2)
+            for item in extra_quant.get(s, []):
+                w_quant(*item)
+            if nxt and i in (1, 2) and q < 2:
+                compress(q + 1, i - 1)
+                rms(q + 1, i - 1)
+            if nxt and i == 1 and q == 2:
+                compress(3, 0)
+                compress(3, 1)
+                rms(3, 0)
+                rms(3, 1)
+            for item in extra_lay.get(s, []):
+                w_lay(*item)
+            k_q(s, 0)
+            if q == 2 and i == 2:
+                norm(3, 0)
+            k_q(s, 1)
+            if nxt and i == 3:
+                l_quant(q + 1)
+            if s + 1 < 16:
+                k_b(s + 1)
+            k_add(s, 0, "g")
+            if n < 16:
+                prod(n // 4, n % 4)
+            k_add(s, 1, "v" if s >= 9 and s % 3 == 0 else "g")
+            if s + 1 < 16:
+                k_a(s + 1)
+            k_store(s)
+            target = min(s + 1 if s < 12 else 4 * s - 34, 16, max(0, s - 3, 2 * s - 8))
+            while v_done < target:
+                v_mm(v_done)
+                v_out(v_done)
+                v_done += 1

@@ -20,7 +20,6 @@ ACT = mybir.ActivationFunctionType
 
 P = 128
 GROUPS = D // 512
-BANKS = {"a": 2, "b": 1, "c": 1, "v": 2, "tr": 2}
 EPS = 1e-6
 
 
@@ -80,8 +79,6 @@ def tile_mla_pa_kernel(tc, x_bytes, x_scale, freqs_cos, freqs_sin, w_kv_compress
         nc.scalar.activation(out=warm_out[:], in_=warm[:], func=ACT.Sqrt)
         ident = keep.tile([P, P], F32, name="ident")
         make_identity(nc, ident[:])
-        ident_bf = keep.tile([P, P], BF16, name="ident_bf")
-        nc.vector.tensor_copy(out=ident_bf[:], in_=ident[:])
 
         rot = keep.tile([P, 2, HALF, 2], F32, name="rot")
         gain = keep.tile([P, R], BF16, name="gain")
@@ -116,25 +113,6 @@ def tile_mla_pa_kernel(tc, x_bytes, x_scale, freqs_cos, freqs_sin, w_kv_compress
             else:
                 lo = (c % 2) * 512 + j * 256
                 lay(eng, out, wu_raw["v", c // 2][:, :, lo : lo + 256].rearrange("p t n -> p n t"))
-
-        def w_turn(kind, c, j, tag, eng):
-            if (kind, c) not in wg:
-                wg[kind, c] = wk.tile([P, 512, 4], BF16, name=f"wg_{kind}{c}", tag="wg", bufs=5, align_bytes=64)
-            if kind == "c":
-                src = wc_raw[c][:].rearrange("q t (p u e) -> q u p e t", u=2, e=2)[:, j]
-            else:
-                src = wu_raw["k", c // 2][:, :, (c % 2) * 512 : (c % 2 + 1) * 512].rearrange("p t (n j) -> p j n t", j=2)[:, 1 - j]
-            bank = ps.tile([P, 1024], BF16, name=f"wt_{kind}{c}_{j}", tag=tag, bufs=BANKS[tag])
-            for h in range(2):
-                if kind == "c":
-                    nc.tensor.matmul(bank[:, h * 512 : (h + 1) * 512].rearrange("q (p e t) -> q p e t", e=2, t=4), lhsT=ident_bf[:], rhs=src[:, h * 64 : (h + 1) * 64], start=True, stop=True)
-                else:
-                    nc.tensor.matmul(bank[:, h * 512 : (h + 1) * 512].rearrange("p (n t) -> p n t", t=4), lhsT=ident_bf[:], rhs=src[:, h * P : (h + 1) * P], start=True, stop=True)
-            out = wg[kind, c][:, j * 256 : (j + 1) * 256, :].rearrange("p n t -> p (n t)")
-            if eng == "v":
-                nc.vector.tensor_copy(out=out, in_=bank[:])
-            else:
-                nc.scalar.copy(out=out, in_=bank[:])
 
         def w_quant(kind, c):
             quant(codes[kind], scales[kind], c * 512, 512, wg[kind, c][:].rearrange("p n t -> p (n t)"))
@@ -299,32 +277,34 @@ def tile_mla_pa_kernel(tc, x_bytes, x_scale, freqs_cos, freqs_sin, w_kv_compress
 
         cast(0, 0, "s")
         cast(0, 2, "s")
+        w_lay("c", 0, 0, "v")
         cast(0, 1, "v")
         cast(0, 3, "v")
-        w_turn("c", 0, 0, "v", "s")
-        w_turn("c", 0, 1, "v", "s")
+        w_lay("c", 0, 1, "v")
         turn(0, 0)
         turn(0, 1)
+        w_lay("c", 1, 0, "s")
+        w_lay("c", 1, 1, "g")
         prod(0, 0)
-        w_turn("c", 1, 0, "a", "s")
-        w_turn("c", 1, 1, "a", "s")
         turn(0, 2)
         prod(0, 1)
-        w_quant("c", 0)
         turn(0, 3)
-        w_turn("c", 2, 0, "v", "s")
-        w_turn("c", 2, 1, "v", "s")
+        w_lay("c", 2, 0, "s")
+        w_lay("c", 2, 1, "g")
+        w_lay("c", 3, 0, "s")
+        w_lay("c", 3, 1, "g")
         prod(0, 2)
-        x_quant(0, 0)
+        w_quant("c", 0)
         w_quant("c", 1)
         cast(1, 0, "s")
         cast(1, 1, "s")
         prod(0, 3)
-        w_turn("c", 3, 0, "a", "s")
-        w_turn("c", 3, 1, "a", "s")
-        w_quant("c", 2)
+        x_quant(0, 0)
         x_quant(0, 1)
+        w_lay("k", 0, 0, "s")
+        w_lay("k", 0, 1, "g")
         turn(1, 0)
+        w_quant("c", 2)
         w_quant("c", 3)
         nc.vector.scalar_tensor_tensor(out=rot[:, :, :, 0], in0=cos[:], scalar=-1.0, in1=sin[:], op0=MULT, op1=SUB)
         nc.vector.scalar_tensor_tensor(out=rot[:, :, :, 1], in0=cos[:], scalar=-1.0, in1=sin[:], op0=MULT, op1=ADD)
@@ -333,10 +313,10 @@ def tile_mla_pa_kernel(tc, x_bytes, x_scale, freqs_cos, freqs_sin, w_kv_compress
         compress(0, 1)
         rms(0, 0)
         rms(0, 1)
+        w_lay("k", 1, 0, "s")
+        w_lay("k", 1, 1, "g")
         cast(1, 2, "s")
         cast(1, 3, "s")
-        w_turn("k", 0, 0, "a", "s")
-        w_turn("k", 0, 1, "a", "s")
         prod(1, 0)
         turn(1, 1)
         turn(1, 2)
@@ -344,20 +324,18 @@ def tile_mla_pa_kernel(tc, x_bytes, x_scale, freqs_cos, freqs_sin, w_kv_compress
         norm(0, 1)
         l_turn(0)
         l_lay(0)
-        w_turn("k", 1, 0, "a", "s")
-        w_turn("k", 1, 1, "a", "s")
-        w_turn("k", 2, 0, "a", "s")
-        w_turn("k", 2, 1, "a", "s")
+        w_lay("k", 2, 0, "s")
+        w_lay("k", 2, 1, "g")
         prod(1, 1)
         w_quant("k", 0)
+        w_lay("k", 3, 0, "s")
+        w_lay("k", 3, 1, "g")
         prod(1, 2)
         l_quant(0)
         w_quant("k", 1)
         k_b(0)
         x_quant(1, 0)
         w_quant("k", 2)
-        w_turn("k", 3, 0, "a", "s")
-        w_turn("k", 3, 1, "a", "s")
         cast(2, 0, "s")
         k_a(0)
 

@@ -69,10 +69,10 @@ def tile_mla_pa_kernel(tc, x_bytes, x_scale, freqs_cos, freqs_sin, w_kv_compress
         load_wu("v", w_v_up, 1)
         load_x(3, 0)
         load_x(3, 1)
-        nc.scalar.dma_start(out=scale[:], in_=x_scale.rearrange("a b (g p t) -> p (a b g) t", p=P, t=4))
-        nc.scalar.dma_start(out=nw[:], in_=kv_norm_w.partition_broadcast(P))
         nc.scalar.dma_start(out=cos[:], in_=freqs_cos.rearrange("(s p) i -> p s i", p=P))
         nc.scalar.dma_start(out=sin[:], in_=freqs_sin.rearrange("(s p) i -> p s i", p=P))
+        nc.scalar.dma_start(out=scale[:], in_=x_scale.rearrange("a b (g p t) -> p (a b g) t", p=P, t=4))
+        nc.scalar.dma_start(out=nw[:], in_=kv_norm_w.partition_broadcast(P))
         warm = keep.tile([P, 1], F32, name="warm")
         nc.vector.memset(warm[:], 1.0)
         warm_out = keep.tile([P, 1], F32, name="warm_out")
@@ -107,12 +107,12 @@ def tile_mla_pa_kernel(tc, x_bytes, x_scale, freqs_cos, freqs_sin, w_kv_compress
                 wg[kind, c] = wk.tile([P, 512, 4], BF16, name=f"wg_{kind}{c}", tag="wg", bufs=5, align_bytes=64)
             out = wg[kind, c][:, j * 256 : (j + 1) * 256, :]
             if kind == "c":
-                lay(eng, out.rearrange("q (p e) t -> q p e t", e=2), wc_raw[c][:].rearrange("q t (p u e) -> q u p e t", u=2, e=2)[:, j])
+                lay(eng, out.rearrange("q (p e) t -> q p t e", e=2), wc_raw[c][:].rearrange("q t (p u e) -> q u p t e", u=2, e=2)[:, j])
             elif kind == "k":
-                lay(eng, out, wu_raw["k", c // 2][:, :, (c % 2) * 512 : (c % 2 + 1) * 512].rearrange("p t (n j) -> p j n t", j=2)[:, 1 - j])
+                lay(eng, out.rearrange("p (c i) t -> p c t i", i=4), wu_raw["k", c // 2][:, :, (c % 2) * 512 : (c % 2 + 1) * 512].rearrange("p t (c i j) -> p j c t i", i=4, j=2)[:, 1 - j])
             else:
                 lo = (c % 2) * 512 + j * 256
-                lay(eng, out, wu_raw["v", c // 2][:, :, lo : lo + 256].rearrange("p t n -> p n t"))
+                lay(eng, out.rearrange("p (c i) t -> p c t i", i=4), wu_raw["v", c // 2][:, :, lo : lo + 256].rearrange("p t (c i) -> p c t i", i=4))
 
         def w_quant(kind, c):
             quant(codes[kind], scales[kind], c * 512, 512, wg[kind, c][:].rearrange("p n t -> p (n t)"))
@@ -144,15 +144,27 @@ def tile_mla_pa_kernel(tc, x_bytes, x_scale, freqs_cos, freqs_sin, w_kv_compress
                     nc.tensor.transpose(tr[:, u, m * P : (m + 1) * P], words[:, 256 * g + u : 256 * (g + 1) : 2], ident[:])
 
         def prod(q, g):
-            if g == 0:
-                xg[q] = wk.tile([P, GROUPS, 256, 4], BF16, name=f"xg{q}", tag="xg", bufs=2, align_bytes=64)
-                x_codes[q] = wk.tile([P, GROUPS * 256], U32, name=f"xc{q}", tag="xc", bufs=2, align_bytes=64)
-                x_scales[q] = wk.tile([P, GROUPS * 256], U8, name=f"xq{q}", tag="xq", bufs=2, align_bytes=64)
+            if q not in xg:
+                x_alloc(q)
             nc.vector.tensor_tensor(
                 out=xg[q][:, g].rearrange("p r (u e) -> p r u e", e=2),
                 in0=trs[q, g][:].bitcast(BF16).rearrange("p u (r e) -> p r u e", e=2),
                 in1=scale[:, g, :].rearrange("p (u e) -> p u e", e=2).unsqueeze(1).to_broadcast([P, 256, 2, 2]),
                 op=MULT)
+
+        def prod_s(q, g):
+            if q not in xg:
+                x_alloc(q)
+            plane = wk.tile([P, 4, 256], BF16, name=f"pl{q}_{g}", tag="plane", bufs=2)
+            tb = trs[q, g][:].bitcast(BF16).rearrange("p u (r e) -> p u r e", e=2)
+            for t in range(4):
+                nc.scalar.activation(out=plane[:, t, :], in_=tb[:, t // 2, :, t % 2], func=ACT.Copy, scale=scale[:, g, t : t + 1])
+            nc.scalar.copy(out=xg[q][:, g].rearrange("p (c i) t -> p c t i", i=4), in_=plane[:].rearrange("p t (c i) -> p c t i", i=4))
+
+        def x_alloc(q):
+            xg[q] = wk.tile([P, GROUPS, 256, 4], BF16, name=f"xg{q}", tag="xg", bufs=2, align_bytes=64)
+            x_codes[q] = wk.tile([P, GROUPS * 256], U32, name=f"xc{q}", tag="xc", bufs=2, align_bytes=64)
+            x_scales[q] = wk.tile([P, GROUPS * 256], U8, name=f"xq{q}", tag="xq", bufs=2, align_bytes=64)
 
         def x_quant(q, i):
             quant(x_codes[q], x_scales[q], i * 512, 512, xg[q][:, 2 * i : 2 * i + 2].rearrange("p g r t -> p (g r t)"))
@@ -239,26 +251,26 @@ def tile_mla_pa_kernel(tc, x_bytes, x_scale, freqs_cos, freqs_sin, w_kv_compress
 
         def k_q(s, hh):
             m = s // 2 % 2
-            qts[s, hh] = wk.tile([P, 512], F32, name=f"qt{s}_{hh}", tag="qt", bufs=5)
+            if hh == 0:
+                qts[s] = wk.tile([P, 1024], F32, name=f"qt{s}", tag="qt", bufs=3)
             nc.vector.tensor_tensor(
-                out=qts[s, hh][:].rearrange("p (h i j) -> p h i j", i=HALF, j=2),
+                out=qts[s][:, hh * 512 : (hh + 1) * 512].rearrange("p (h i j) -> p h i j", i=HALF, j=2),
                 in0=az[s, hh][:].rearrange("p (j h i) -> p h i j", j=2, i=HALF),
                 in1=rot[:, m].unsqueeze(1).to_broadcast([P, 4, HALF, 2]), op=MULT)
 
         oks = {}
 
-        def k_add(s, hh, eng):
-            if hh == 0:
+        def k_add(s, eng, lo=0, hi=512):
+            if s not in oks:
                 oks[s] = wk.tile([P, 1024], F32, name=f"ok{s}", tag="ok", bufs=4)
             e = nc.gpsimd if eng == "g" else nc.vector
             e.tensor_tensor(
-                out=oks[s][:, hh * 512 : (hh + 1) * 512].rearrange("p (n j) -> p n j", j=2),
-                in0=pts[s][:, hh * 256 : (hh + 1) * 256].unsqueeze(2).to_broadcast([P, 256, 2]),
-                in1=qts[s, hh][:].rearrange("p (n j) -> p n j", j=2), op=ADD)
+                out=oks[s][:, 2 * lo : 2 * hi].rearrange("p (n j) -> p n j", j=2), in0=pts[s][:, lo:hi].unsqueeze(2).to_broadcast([P, hi - lo, 2]),
+                in1=qts[s][:, 2 * lo : 2 * hi].rearrange("p (n j) -> p n j", j=2), op=ADD)
 
-        def k_store(s):
+        def k_store(s, lo=0, hi=1024):
             q, m, half = s // 4, s // 2 % 2, s % 2
-            nc.sync.dma_start(out=out_0[q, m * P : (m + 1) * P].rearrange("s h d -> s (h d)")[:, half * 1024 : (half + 1) * 1024], in_=oks[s][:])
+            nc.sync.dma_start(out=out_0[q, m * P : (m + 1) * P].rearrange("s h d -> s (h d)")[:, half * 1024 + lo : half * 1024 + hi], in_=oks[s][:, lo:hi])
 
         vs = {}
 
@@ -277,10 +289,13 @@ def tile_mla_pa_kernel(tc, x_bytes, x_scale, freqs_cos, freqs_sin, w_kv_compress
 
         cast(0, 0, "s")
         cast(0, 2, "s")
+        nc.vector.scalar_tensor_tensor(out=rot[:, :, :, 0], in0=cos[:], scalar=-1.0, in1=sin[:], op0=MULT, op1=SUB)
+        nc.vector.scalar_tensor_tensor(out=rot[:, :, :, 1], in0=cos[:], scalar=-1.0, in1=sin[:], op0=MULT, op1=ADD)
         w_lay("c", 0, 0, "v")
         cast(0, 1, "v")
         cast(0, 3, "v")
         w_lay("c", 0, 1, "v")
+        nc.vector.tensor_copy(out=gain[:].rearrange("q (u p e) -> q u p e", u=2, e=2), in_=nw[:].rearrange("q (p u e) -> q u p e", u=2, e=2))
         turn(0, 0)
         turn(0, 1)
         w_lay("c", 1, 0, "s")
@@ -292,29 +307,26 @@ def tile_mla_pa_kernel(tc, x_bytes, x_scale, freqs_cos, freqs_sin, w_kv_compress
         w_lay("c", 2, 0, "s")
         w_lay("c", 2, 1, "g")
         w_lay("c", 3, 0, "s")
-        w_lay("c", 3, 1, "g")
+        w_lay("c", 3, 1, "s")
         prod(0, 2)
         w_quant("c", 0)
-        w_quant("c", 1)
         cast(1, 0, "s")
         cast(1, 1, "s")
         prod(0, 3)
+        w_quant("c", 1)
         x_quant(0, 0)
         x_quant(0, 1)
         w_lay("k", 0, 0, "s")
-        w_lay("k", 0, 1, "g")
+        w_lay("k", 0, 1, "s")
         turn(1, 0)
         w_quant("c", 2)
         w_quant("c", 3)
-        nc.vector.scalar_tensor_tensor(out=rot[:, :, :, 0], in0=cos[:], scalar=-1.0, in1=sin[:], op0=MULT, op1=SUB)
-        nc.vector.scalar_tensor_tensor(out=rot[:, :, :, 1], in0=cos[:], scalar=-1.0, in1=sin[:], op0=MULT, op1=ADD)
-        nc.vector.tensor_copy(out=gain[:].rearrange("q (u p e) -> q u p e", u=2, e=2), in_=nw[:].rearrange("q (p u e) -> q u p e", u=2, e=2))
         compress(0, 0)
         compress(0, 1)
+        w_lay("k", 1, 0, "s")
+        w_lay("k", 1, 1, "s")
         rms(0, 0)
         rms(0, 1)
-        w_lay("k", 1, 0, "s")
-        w_lay("k", 1, 1, "g")
         cast(1, 2, "s")
         cast(1, 3, "s")
         prod(1, 0)
@@ -336,59 +348,77 @@ def tile_mla_pa_kernel(tc, x_bytes, x_scale, freqs_cos, freqs_sin, w_kv_compress
         k_b(0)
         x_quant(1, 0)
         w_quant("k", 2)
+        turn(1, 3)
+        prod(1, 3)
+        x_quant(1, 1)
         cast(2, 0, "s")
+        cast(2, 1, "s")
         k_a(0)
 
-        extra_lay = {0: [("v", 0, 0, "s")], 1: [("v", 0, 1, "s"), ("v", 1, 0, "s")], 2: [("v", 1, 1, "s"), ("v", 2, 0, "s")], 3: [("v", 2, 1, "s"), ("v", 3, 0, "s")], 4: [("v", 3, 1, "s")]}
-        extra_quant = {0: [("k", 3)], 2: [("v", 0)], 3: [("v", 1)], 4: [("v", 2)], 5: [("v", 3)]}
+        extra_lay = {0: [("v", 0, 0, "s"), ("v", 0, 1, "s")], 1: [("v", 1, 0, "s"), ("v", 1, 1, "s")], 2: [("v", 2, 0, "s"), ("v", 2, 1, "s")], 3: [("v", 3, 0, "s"), ("v", 3, 1, "s")]}
+        extra_quant = {1: [("v", 0)], 3: [("v", 1)], 5: [("v", 2), ("v", 3)]}
+        on_s = {9, 11, 13, 15}
         v_done = 0
-        LEAD = 7
         for s in range(16):
             q, i = s // 4, s % 4
             nxt = q + 1 < B
-            n = s + LEAD
-            c = s + LEAD + 2
+            c = s + 10
             if c < 16:
                 cast(c // 4, c % 4, "s")
-            if nxt and i >= 2 and (q < 2 or i == 3):
-                norm(q + 1, i - 2)
-            if nxt and i == 3:
-                l_turn(q + 1)
-                l_lay(q + 1)
-            if n < 16:
-                turn(n // 4, n % 4)
-            k_p(s)
-            pend = n - 1
-            if pend < 16 and pend % 2 == 1:
-                x_quant(pend // 4, pend % 4 // 2)
-            for item in extra_quant.get(s, []):
-                w_quant(*item)
-            if nxt and i in (1, 2) and q < 2:
-                compress(q + 1, i - 1)
-                rms(q + 1, i - 1)
-            if nxt and i == 1 and q == 2:
-                compress(3, 0)
-                compress(3, 1)
-                rms(3, 0)
-                rms(3, 1)
+            if q + 2 < B and i % 2 == 0:
+                for g in (i, i + 1):
+                    turn(q + 2, g)
+                    if 4 * q + 8 + g in on_s:
+                        prod_s(q + 2, g)
             for item in extra_lay.get(s, []):
                 w_lay(*item)
+            k_p(s)
             k_q(s, 0)
-            if q == 2 and i == 2:
-                norm(3, 0)
             k_q(s, 1)
+            if s == 0:
+                w_quant("k", 3)
             if nxt and i == 3:
                 l_quant(q + 1)
             if s + 1 < 16:
                 k_b(s + 1)
-            k_add(s, 0, "g")
-            if n < 16:
-                prod(n // 4, n % 4)
-            k_add(s, 1, "v" if s >= 9 and s % 3 == 0 else "g")
+            if nxt and i in (1, 2):
+                norm(q + 1, i - 1)
+            if nxt and i < 2:
+                compress(q + 1, i)
+                rms(q + 1, i)
+            if nxt and i == 2:
+                l_turn(q + 1)
+                l_lay(q + 1)
+            if i % 2 == 0:
+                if s < 9:
+                    k_add(s, "g")
+                else:
+                    k_add(s, "g", 0, 256)
+                if q + 2 < B:
+                    for g in (i, i + 1):
+                        if 4 * q + 8 + g not in on_s:
+                            prod(q + 2, g)
+                if s < 9:
+                    k_store(s)
+            else:
+                if s - 1 >= 9:
+                    k_add(s - 1, "v", 256, 512)
+                    k_store(s - 1)
+                if s == 15:
+                    k_add(s, "v", 0, 256)
+                    k_store(s, 0, 512)
+                    k_add(s, "v", 256, 512)
+                    k_store(s, 512, 1024)
+                else:
+                    k_add(s, "v")
+                    k_store(s)
+                if q + 2 < B:
+                    x_quant(q + 2, i // 2)
+            for item in extra_quant.get(s, []):
+                w_quant(*item)
             if s + 1 < 16:
                 k_a(s + 1)
-            k_store(s)
-            target = min(s + 1 if s < 12 else 4 * s - 34, 16, max(0, s - 3, 2 * s - 8))
+            target = min(16, 4 * (q + 1), max(0, 2 * (s - 4)), v_done + 2)
             while v_done < target:
                 v_mm(v_done)
                 v_out(v_done)

@@ -31,7 +31,6 @@ def tile_mla_pa_kernel(tc, x_bytes, x_scale, freqs_cos, freqs_sin, w_kv_compress
         wk = ctx.enter_context(tc.tile_pool(name="wk", bufs=1))
         ps = ctx.enter_context(tc.psum_pool(name="ps", bufs=1))
 
-        ctx.enter_context(tc.manual_schedule())
         xb = {}
 
         def load_x(q, m):
@@ -55,13 +54,14 @@ def tile_mla_pa_kernel(tc, x_bytes, x_scale, freqs_cos, freqs_sin, w_kv_compress
         sin = keep.tile([P, 2, HALF], BF16, name="sin")
         nw = keep.tile([P, R], BF16, name="nw")
         load_x(0, 0)
-        load_wc(0)
         load_x(0, 1)
+        load_wc(0)
         for g in range(1, GROUPS):
             load_wc(g)
         load_x(1, 0)
         load_x(1, 1)
         load_wu("k", w_k_up, 0)
+        nc.sync.dma_start(out=nw[:], in_=kv_norm_w.partition_broadcast(P))
         load_wu("k", w_k_up, 1)
         load_wu("v", w_v_up, 0)
         load_x(2, 0)
@@ -72,11 +72,10 @@ def tile_mla_pa_kernel(tc, x_bytes, x_scale, freqs_cos, freqs_sin, w_kv_compress
         nc.scalar.dma_start(out=cos[:], in_=freqs_cos.rearrange("(s p) i -> p s i", p=P))
         nc.scalar.dma_start(out=sin[:], in_=freqs_sin.rearrange("(s p) i -> p s i", p=P))
         nc.scalar.dma_start(out=scale[:], in_=x_scale.rearrange("a b (g p t) -> p (a b g) t", p=P, t=4))
-        nc.scalar.dma_start(out=nw[:], in_=kv_norm_w.partition_broadcast(P))
         warm = keep.tile([P, 1], F32, name="warm")
         nc.vector.memset(warm[:], 1.0)
         warm_out = keep.tile([P, 1], F32, name="warm_out")
-        nc.scalar.activation(out=warm_out[:], in_=warm[:], func=ACT.Sqrt)
+        nc.scalar.activation(out=warm_out[:], in_=warm[:], func=ACT.Abs_reciprocal_sqrt)
         ident = keep.tile([P, P], F32, name="ident")
         make_identity(nc, ident[:])
 
@@ -159,7 +158,7 @@ def tile_mla_pa_kernel(tc, x_bytes, x_scale, freqs_cos, freqs_sin, w_kv_compress
             tb = trs[q, g][:].bitcast(BF16).rearrange("p u (r e) -> p u r e", e=2)
             for t in range(4):
                 nc.scalar.activation(out=plane[:, t, :], in_=tb[:, t // 2, :, t % 2], func=ACT.Copy, scale=scale[:, g, t : t + 1])
-            nc.scalar.copy(out=xg[q][:, g].rearrange("p (c i) t -> p c t i", i=4), in_=plane[:].rearrange("p t (c i) -> p c t i", i=4))
+            lay("s", xg[q][:, g].rearrange("p (c i) t -> p c t i", i=4), plane[:].rearrange("p t (c i) -> p c t i", i=4))
 
         def x_alloc(q):
             xg[q] = wk.tile([P, GROUPS, 256, 4], BF16, name=f"xg{q}", tag="xg", bufs=2, align_bytes=64)
@@ -193,13 +192,11 @@ def tile_mla_pa_kernel(tc, x_bytes, x_scale, freqs_cos, freqs_sin, w_kv_compress
             ss = wk.tile([P, 1], F32, name=f"ss{q}_{m}", tag="ss", bufs=4)
             nc.scalar.activation(out=junk[:], in_=cs[q, m][:], func=ACT.Square, accum_out=ss[:])
             sds[q, m] = wk.tile([P, 1], F32, name=f"sd{q}_{m}", tag="sd", bufs=4)
-            nc.scalar.activation(out=sds[q, m][:], in_=ss[:], func=ACT.Sqrt, bias=EPS, scale=1.0 / R)
+            nc.scalar.activation(out=sds[q, m][:], in_=ss[:], func=ACT.Abs_reciprocal_sqrt, bias=EPS, scale=1.0 / R)
 
         def norm(q, m):
-            rs = wk.tile([P, 1], F32, name=f"rs{q}_{m}", tag="rs", bufs=4)
-            nc.vector.reciprocal(rs[:], sds[q, m][:])
             lat[q, m] = wk.tile([P, R], BF16, name=f"lat{q}_{m}", tag="lat", bufs=4)
-            nc.vector.scalar_tensor_tensor(out=lat[q, m][:], in0=cs[q, m][:], scalar=rs[:], in1=gain[:], op0=MULT, op1=MULT)
+            nc.vector.scalar_tensor_tensor(out=lat[q, m][:], in0=cs[q, m][:], scalar=sds[q, m][:], in1=gain[:], op0=MULT, op1=MULT)
 
         def l_turn(q):
             lts[q] = ps.tile([P, 2, 256], F32, name=f"lt{q}", tag="tr", bufs=2)
@@ -288,25 +285,25 @@ def tile_mla_pa_kernel(tc, x_bytes, x_scale, freqs_cos, freqs_sin, w_kv_compress
             nc.sync.dma_start(out=out_1[q, m * P : (m + 1) * P].rearrange("s h d -> s (h d)")[:, half * 1024 : (half + 1) * 1024], in_=ov[:])
 
         cast(0, 0, "s")
-        cast(0, 2, "s")
+        cast(0, 2, "v")
         nc.vector.scalar_tensor_tensor(out=rot[:, :, :, 0], in0=cos[:], scalar=-1.0, in1=sin[:], op0=MULT, op1=SUB)
         nc.vector.scalar_tensor_tensor(out=rot[:, :, :, 1], in0=cos[:], scalar=-1.0, in1=sin[:], op0=MULT, op1=ADD)
         w_lay("c", 0, 0, "v")
         cast(0, 1, "v")
-        cast(0, 3, "v")
-        w_lay("c", 0, 1, "v")
+        cast(0, 3, "s")
+        w_lay("c", 0, 1, "g")
         nc.vector.tensor_copy(out=gain[:].rearrange("q (u p e) -> q u p e", u=2, e=2), in_=nw[:].rearrange("q (p u e) -> q u p e", u=2, e=2))
         turn(0, 0)
         turn(0, 1)
-        w_lay("c", 1, 0, "s")
-        w_lay("c", 1, 1, "g")
+        w_lay("c", 1, 0, "g")
+        w_lay("c", 1, 1, "s")
         prod(0, 0)
         turn(0, 2)
         prod(0, 1)
         turn(0, 3)
-        w_lay("c", 2, 0, "s")
-        w_lay("c", 2, 1, "g")
-        w_lay("c", 3, 0, "s")
+        w_lay("c", 2, 0, "g")
+        w_lay("c", 2, 1, "s")
+        w_lay("c", 3, 0, "g")
         w_lay("c", 3, 1, "s")
         prod(0, 2)
         w_quant("c", 0)
@@ -337,11 +334,11 @@ def tile_mla_pa_kernel(tc, x_bytes, x_scale, freqs_cos, freqs_sin, w_kv_compress
         l_turn(0)
         l_lay(0)
         w_lay("k", 2, 0, "s")
-        w_lay("k", 2, 1, "g")
+        w_lay("k", 2, 1, "s")
         prod(1, 1)
         w_quant("k", 0)
         w_lay("k", 3, 0, "s")
-        w_lay("k", 3, 1, "g")
+        w_lay("k", 3, 1, "s")
         prod(1, 2)
         l_quant(0)
         w_quant("k", 1)
@@ -355,16 +352,17 @@ def tile_mla_pa_kernel(tc, x_bytes, x_scale, freqs_cos, freqs_sin, w_kv_compress
         cast(2, 1, "s")
         k_a(0)
 
-        extra_lay = {0: [("v", 0, 0, "s"), ("v", 0, 1, "s")], 1: [("v", 1, 0, "s"), ("v", 1, 1, "s")], 2: [("v", 2, 0, "s"), ("v", 2, 1, "s")], 3: [("v", 3, 0, "s"), ("v", 3, 1, "s")]}
-        extra_quant = {1: [("v", 0)], 3: [("v", 1)], 5: [("v", 2), ("v", 3)]}
-        on_s = {9, 11, 13, 15}
+        extra_lay = {2: [('v', 0, 0, 's'), ('v', 0, 1, 'v'), ('v', 1, 0, 's'), ('v', 1, 1, 'v')], 3: [('v', 2, 0, 's'), ('v', 2, 1, 'v'), ('v', 3, 0, 's'), ('v', 3, 1, 'g')]}
+        extra_quant = {3: [('v', 0), ('v', 1), ('v', 2), ('v', 3)]}
+        on_s = {9,11,15}
         v_done = 0
+        POL = ['gg', 'gg', 'gg', 'vv', 'gg', 'gg', 'gg', 'vv', 'gg', 'gg', 'gg', 'vv', 'gg', 'gg', 'vv', 'vv']
+        VT = [0, 0, 0, 2, 4, 6, 8, 8, 12, 12, 12, 12, 16, 16, 16, 16]
         for s in range(16):
             q, i = s // 4, s % 4
             nxt = q + 1 < B
-            c = s + 10
-            if c < 16:
-                cast(c // 4, c % 4, "s")
+            if s + 10 < 16:
+                cast((s + 10) // 4, (s + 10) % 4, "s")
             if q + 2 < B and i % 2 == 0:
                 for g in (i, i + 1):
                     turn(q + 2, g)
@@ -389,36 +387,28 @@ def tile_mla_pa_kernel(tc, x_bytes, x_scale, freqs_cos, freqs_sin, w_kv_compress
             if nxt and i == 2:
                 l_turn(q + 1)
                 l_lay(q + 1)
-            if i % 2 == 0:
-                if s < 9:
-                    k_add(s, "g")
-                else:
-                    k_add(s, "g", 0, 256)
-                if q + 2 < B:
-                    for g in (i, i + 1):
-                        if 4 * q + 8 + g not in on_s:
-                            prod(q + 2, g)
-                if s < 9:
-                    k_store(s)
+            for piece, eng in enumerate(POL[s]):
+                if eng == "g":
+                    k_add(s, "g", piece * 256, (piece + 1) * 256)
+            if i % 2 == 0 and q + 2 < B:
+                for g in (i, i + 1):
+                    if 4 * q + 8 + g not in on_s:
+                        prod(q + 2, g)
+            for piece, eng in enumerate(POL[s]):
+                if eng == "v":
+                    k_add(s, "v", piece * 256, (piece + 1) * 256)
+            if s == 15:
+                k_store(s, 0, 512)
+                k_store(s, 512, 1024)
             else:
-                if s - 1 >= 9:
-                    k_add(s - 1, "v", 256, 512)
-                    k_store(s - 1)
-                if s == 15:
-                    k_add(s, "v", 0, 256)
-                    k_store(s, 0, 512)
-                    k_add(s, "v", 256, 512)
-                    k_store(s, 512, 1024)
-                else:
-                    k_add(s, "v")
-                    k_store(s)
-                if q + 2 < B:
-                    x_quant(q + 2, i // 2)
+                k_store(s)
+            if i % 2 == 1 and q + 2 < B:
+                x_quant(q + 2, i // 2)
             for item in extra_quant.get(s, []):
                 w_quant(*item)
             if s + 1 < 16:
                 k_a(s + 1)
-            target = min(16, 4 * (q + 1), max(0, 2 * (s - 4)), v_done + 2)
+            target = VT[s]
             while v_done < target:
                 v_mm(v_done)
                 v_out(v_done)

@@ -352,9 +352,9 @@ def tile_mla_pa_kernel(tc, x_bytes, x_scale, freqs_cos, freqs_sin, w_kv_compress
         cast(2, 1, "s")
         k_a(0)
 
-        extra_lay = {2: [('v', 0, 0, 's'), ('v', 0, 1, 'v'), ('v', 1, 0, 's'), ('v', 1, 1, 'v')], 3: [('v', 2, 0, 's'), ('v', 2, 1, 'v'), ('v', 3, 0, 's'), ('v', 3, 1, 'g')]}
-        extra_quant = {3: [('v', 0), ('v', 1), ('v', 2), ('v', 3)]}
-        on_s = {9,11,15}
+        extra_lay = {0: [('v', 0, 0, 's'), ('v', 0, 1, 'v'), ('v', 1, 0, 's'), ('v', 1, 1, 'v')], 1: [('v', 2, 0, 's'), ('v', 2, 1, 'v'), ('v', 3, 0, 'g'), ('v', 3, 1, 's')]}
+        extra_quant = {1: [('v', 0), ('v', 1), ('v', 2), ('v', 3)]}
+        on_s = {10,11,15}
         v_done = 0
         POL = ['gg', 'gg', 'gg', 'vv', 'gg', 'gg', 'gg', 'vv', 'gg', 'gg', 'gg', 'vv', 'gg', 'gg', 'vv', 'vv']
         VT = [0, 0, 0, 2, 4, 6, 8, 8, 12, 12, 12, 12, 16, 16, 16, 16]

from contextlib import ExitStack

import concourse.mybir as mybir
from concourse.masks import make_identity

B, S, D, H, DH, R = 4, 256, 2048, 16, 128, 512
HALF = DH // 2
FLOPS = 2 * B * S * R * (D + 2 * H * DH)

F32 = mybir.dt.float32
BF16 = mybir.dt.bfloat16
U32 = mybir.dt.uint32
U8 = mybir.dt.uint8
FP8 = mybir.dt.float8_e4m3fn
FP8X4 = mybir.dt.float8_e4m3fn_x4
MULT = mybir.AluOpType.mult
ADD = mybir.AluOpType.add
SUB = mybir.AluOpType.subtract
ACT = mybir.ActivationFunctionType

P = 128
GROUPS = D // 512
EPS = 1e-6


def tile_mla_pa_kernel(tc, x_bytes, x_scale, freqs_cos, freqs_sin, w_kv_compress, kv_norm_w, w_k_up, w_v_up, out_0, out_1):
    nc = tc.nc
    with ExitStack() as ctx:
        keep = ctx.enter_context(tc.tile_pool(name="keep", bufs=1))
        ld = ctx.enter_context(tc.tile_pool(name="ld", bufs=1))
        wk = ctx.enter_context(tc.tile_pool(name="wk", bufs=1))
        ps = ctx.enter_context(tc.psum_pool(name="ps", bufs=1))

        xb = {}

        def load_x(q, m):
            xb[q, m] = ld.tile([P, D], U8, name=f"xb{q}_{m}", tag="xb", bufs=8)
            nc.sync.dma_start(out=xb[q, m][:], in_=x_bytes[q, m * P : (m + 1) * P, :])

        wc_raw = {}

        def load_wc(g):
            wc_raw[g] = ld.tile([P, 4, R], BF16, name=f"wcr{g}", tag="wcr", bufs=4)
            nc.sync.dma_start(out=wc_raw[g][:], in_=w_kv_compress[g * 512 : (g + 1) * 512, :].rearrange("(p t) n -> p t n", t=4))

        wu_raw = {}

        def load_wu(kind, w, c):
            wu_raw[kind, c] = ld.tile([P, 4, 1024], BF16, name=f"wr{kind}{c}", tag="wr", bufs=4)
            nc.sync.dma_start(out=wu_raw[kind, c][:], in_=w.rearrange("(p t) n -> p t n", t=4)[:, :, c * 1024 : (c + 1) * 1024])

        scale = keep.tile([P, GROUPS, 4], F32, name="scale")
        cos = keep.tile([P, 2, HALF], BF16, name="cos")
        sin = keep.tile([P, 2, HALF], BF16, name="sin")
        nw = keep.tile([P, R], BF16, name="nw")
        load_x(0, 0)
        load_x(0, 1)
        load_wc(0)
        for g in range(1, GROUPS):
            load_wc(g)
        load_x(1, 0)
        load_x(1, 1)
        load_wu("k", w_k_up, 0)
        nc.sync.dma_start(out=nw[:], in_=kv_norm_w.partition_broadcast(P))
        load_wu("k", w_k_up, 1)
        load_wu("v", w_v_up, 0)
        load_x(2, 0)
        load_x(2, 1)
        load_wu("v", w_v_up, 1)
        load_x(3, 0)
        load_x(3, 1)
        nc.scalar.dma_start(out=cos[:], in_=freqs_cos.rearrange("(s p) i -> p s i", p=P))
        nc.scalar.dma_start(out=sin[:], in_=freqs_sin.rearrange("(s p) i -> p s i", p=P))
        nc.scalar.dma_start(out=scale[:], in_=x_scale.rearrange("a b (g p t) -> p (a b g) t", p=P, t=4))
        warm = keep.tile([P, 1], F32, name="warm")
        nc.vector.memset(warm[:], 1.0)
        warm_out = keep.tile([P, 1], F32, name="warm_out")
        nc.scalar.activation(out=warm_out[:], in_=warm[:], func=ACT.Abs_reciprocal_sqrt)
        ident = keep.tile([P, P], F32, name="ident")
        make_identity(nc, ident[:])

        rot = keep.tile([P, 2, HALF, 2], F32, name="rot")
        gain = keep.tile([P, R], BF16, name="gain")

        def lay(eng, out, in_):
            if eng == "v":
                nc.vector.tensor_copy(out=out, in_=in_)
            elif eng == "g":
                nc.gpsimd.tensor_scalar(out=out, in0=in_, scalar1=1.0, scalar2=0.0, op0=MULT, op1=ADD)
            else:
                nc.scalar.copy(out=out, in_=in_)

        codes = {}
        scales = {}
        for kind, width in (("c", GROUPS * R), ("k", H * DH), ("v", H * DH)):
            codes[kind] = keep.tile([P, width], U32, name=f"codes_{kind}", align_bytes=64)
            scales[kind] = keep.tile([P, width], U8, name=f"scales_{kind}", align_bytes=64)

        def quant(cd, sc, lo, width, grouped):
            nc.vector.quantize_mx(out=cd[:, lo : lo + width].bitcast(FP8X4), scales=sc[:, lo : lo + width], in_=grouped)

        wg = {}

        def w_lay(kind, c, j, eng):
            if (kind, c) not in wg:
                wg[kind, c] = wk.tile([P, 512, 4], BF16, name=f"wg_{kind}{c}", tag="wg", bufs=5, align_bytes=64)
            out = wg[kind, c][:, j * 256 : (j + 1) * 256, :]
            if kind == "c":
                lay(eng, out.rearrange("q (p e) t -> q p t e", e=2), wc_raw[c][:].rearrange("q t (p u e) -> q u p t e", u=2, e=2)[:, j])
            elif kind == "k":
                lay(eng, out.rearrange("p (c i) t -> p c t i", i=4), wu_raw["k", c // 2][:, :, (c % 2) * 512 : (c % 2 + 1) * 512].rearrange("p t (c i j) -> p j c t i", i=4, j=2)[:, 1 - j])
            else:
                lo = (c % 2) * 512 + j * 256
                lay(eng, out.rearrange("p (c i) t -> p c t i", i=4), wu_raw["v", c // 2][:, :, lo : lo + 256].rearrange("p t (c i) -> p c t i", i=4))

        def w_quant(kind, c):
            quant(codes[kind], scales[kind], c * 512, 512, wg[kind, c][:].rearrange("p n t -> p (n t)"))

        xs = {}
        xg = {}
        x_codes = {}
        x_scales = {}

        def cast(q, k, eng):
            m, h = k % 2, k // 2
            if k < 2:
                xs[q, m] = wk.tile([P, D], BF16, name=f"xs{q}_{m}", tag="xs", bufs=4)
            out = xs[q, m][:, h * 1024 : (h + 1) * 1024]
            in_ = xb[q, m][:, h * 1024 : (h + 1) * 1024].bitcast(FP8)
            if eng == "v":
                nc.vector.tensor_copy(out=out, in_=in_)
            else:
                nc.scalar.copy(out=out, in_=in_)

        trs = {}

        def turn(q, g):
            tr = ps.tile([P, 2, 256], F32, name=f"tr{q}_{g}", tag="tr", bufs=2)
            trs[q, g] = tr
            for m in range(2):
                words = xs[q, m][:].bitcast(F32)
                for u in range(2):
                    nc.tensor.transpose(tr[:, u, m * P : (m + 1) * P], words[:, 256 * g + u : 256 * (g + 1) : 2], ident[:])

        def prod(q, g):
            if q not in xg:
                x_alloc(q)
            nc.vector.tensor_tensor(
                out=xg[q][:, g].rearrange("p r (u e) -> p r u e", e=2),
                in0=trs[q, g][:].bitcast(BF16).rearrange("p u (r e) -> p r u e", e=2),
                in1=scale[:, g, :].rearrange("p (u e) -> p u e", e=2).unsqueeze(1).to_broadcast([P, 256, 2, 2]),
                op=MULT)

        def prod_s(q, g):
            if q not in xg:
                x_alloc(q)
            plane = wk.tile([P, 4, 256], BF16, name=f"pl{q}_{g}", tag="plane", bufs=2)
            tb = trs[q, g][:].bitcast(BF16).rearrange("p u (r e) -> p u r e", e=2)
            for t in range(4):
                nc.scalar.activation(out=plane[:, t, :], in_=tb[:, t // 2, :, t % 2], func=ACT.Copy, scale=scale[:, g, t : t + 1])
            lay("s", xg[q][:, g].rearrange("p (c i) t -> p c t i", i=4), plane[:].rearrange("p t (c i) -> p c t i", i=4))

        def x_alloc(q):
            xg[q] = wk.tile([P, GROUPS, 256, 4], BF16, name=f"xg{q}", tag="xg", bufs=2, align_bytes=64)
            x_codes[q] = wk.tile([P, GROUPS * 256], U32, name=f"xc{q}", tag="xc", bufs=2, align_bytes=64)
            x_scales[q] = wk.tile([P, GROUPS * 256], U8, name=f"xq{q}", tag="xq", bufs=2, align_bytes=64)

        def x_quant(q, i):
            quant(x_codes[q], x_scales[q], i * 512, 512, xg[q][:, 2 * i : 2 * i + 2].rearrange("p g r t -> p (g r t)"))

        cs = {}
        sds = {}
        lat = {}
        l_codes = {}
        l_scales = {}
        lts = {}
        lgs = {}

        def compress(q, m):
            tag = "c" if m == 0 or q in (1, 2) else "v" if q == 0 else "tr"
            c = ps.tile([P, R], F32, name=f"c{q}_{m}", tag=tag, bufs=1 if tag == "c" else 2)
            cs[q, m] = c
            for g in range(GROUPS):
                lo = g * 256 + m * P
                nc.tensor.matmul_mx(
                    out=c[:], lhsT=x_codes[q][:, lo : lo + P].bitcast(FP8X4), lhsT_scale=x_scales[q][:, lo : lo + P],
                    rhs=codes["c"][:, g * R : (g + 1) * R].bitcast(FP8X4), rhs_scale=scales["c"][:, g * R : (g + 1) * R],
                    start=(g == 0), stop=(g == GROUPS - 1))

        def rms(q, m):
            junk = wk.tile([P, R], BF16, name=f"junk{q}_{m}", tag="junk", bufs=2)
            ss = wk.tile([P, 1], F32, name=f"ss{q}_{m}", tag="ss", bufs=4)
            nc.scalar.activation(out=junk[:], in_=cs[q, m][:], func=ACT.Square, accum_out=ss[:])
            sds[q, m] = wk.tile([P, 1], F32, name=f"sd{q}_{m}", tag="sd", bufs=4)
            nc.scalar.activation(out=sds[q, m][:], in_=ss[:], func=ACT.Abs_reciprocal_sqrt, bias=EPS, scale=1.0 / R)

        def norm(q, m):
            lat[q, m] = wk.tile([P, R], BF16, name=f"lat{q}_{m}", tag="lat", bufs=4)
            nc.vector.scalar_tensor_tensor(out=lat[q, m][:], in0=cs[q, m][:], scalar=sds[q, m][:], in1=gain[:], op0=MULT, op1=MULT)

        def l_turn(q):
            lts[q] = ps.tile([P, 2, 256], F32, name=f"lt{q}", tag="tr", bufs=2)
            for m in range(2):
                words = lat[q, m][:].bitcast(F32)
                for u in range(2):
                    nc.tensor.transpose(lts[q][:, u, m * P : (m + 1) * P], words[:, u * P : (u + 1) * P], ident[:])

        def l_lay(q):
            lgs[q] = wk.tile([P, 256, 4], BF16, name=f"lg{q}", tag="lg", bufs=2, align_bytes=64)
            nc.scalar.copy(out=lgs[q][:].rearrange("p r t -> p (r t)").bitcast(F32).rearrange("p (r u) -> p r u", u=2), in_=lts[q][:].rearrange("p u r -> p r u"))

        def l_quant(q):
            l_codes[q] = wk.tile([P, 256], U32, name=f"lc{q}", tag="lc", bufs=4, align_bytes=64)
            l_scales[q] = wk.tile([P, 256], U8, name=f"lq{q}", tag="lq", bufs=4, align_bytes=64)
            quant(l_codes[q], l_scales[q], 0, 256, lgs[q][:].rearrange("p r t -> p (r t)"))

        def up(q, m, kind, lo, width, out, start, stop):
            nc.tensor.matmul_mx(
                out=out, lhsT=l_codes[q][:, m * P : (m + 1) * P].bitcast(FP8X4), lhsT_scale=l_scales[q][:, m * P : (m + 1) * P],
                rhs=codes[kind][:, lo : lo + width].bitcast(FP8X4), rhs_scale=scales[kind][:, lo : lo + width], start=start, stop=stop)

        bs = {}
        az = {}

        def k_b(s):
            q, m, half = s // 4, s // 2 % 2, s % 2
            bs[s] = ps.tile([P, 512], F32, name=f"b{s}", tag="b", bufs=1)
            for hh in range(2):
                lo = (2 * half + hh) * 512
                up(q, m, "k", lo, 256, bs[s][:, hh * 256 : (hh + 1) * 256], True, False)
                up(q, m, "k", lo + 256, 256, bs[s][:, hh * 256 : (hh + 1) * 256], False, True)

        def k_a(s):
            q, m, half = s // 4, s // 2 % 2, s % 2
            for hh in range(2):
                az[s, hh] = ps.tile([P, 512], F32, name=f"a{s}_{hh}", tag="a", bufs=2)
                up(q, m, "k", (2 * half + hh) * 512, 512, az[s, hh][:], True, True)

        pts = {}
        qts = {}

        def k_p(s):
            m = s // 2 % 2
            pts[s] = wk.tile([P, 512], F32, name=f"pt{s}", tag="pt", bufs=3)
            nc.vector.tensor_tensor(
                out=pts[s][:].rearrange("p (h i) -> p h i", i=HALF), in0=bs[s][:].rearrange("p (h i) -> p h i", i=HALF),
                in1=cos[:, m, :].unsqueeze(1).to_broadcast([P, 8, HALF]), op=MULT)

        def k_q(s, hh):
            m = s // 2 % 2
            if hh == 0:
                qts[s] = wk.tile([P, 1024], F32, name=f"qt{s}", tag="qt", bufs=3)
            nc.vector.tensor_tensor(
                out=qts[s][:, hh * 512 : (hh + 1) * 512].rearrange("p (h i j) -> p h i j", i=HALF, j=2),
                in0=az[s, hh][:].rearrange("p (j h i) -> p h i j", j=2, i=HALF),
                in1=rot[:, m].unsqueeze(1).to_broadcast([P, 4, HALF, 2]), op=MULT)

        oks = {}

        def k_add(s, eng, lo=0, hi=512):
            if s not in oks:
                oks[s] = wk.tile([P, 1024], F32, name=f"ok{s}", tag="ok", bufs=4)
            e = nc.gpsimd if eng == "g" else nc.vector
            e.tensor_tensor(
                out=oks[s][:, 2 * lo : 2 * hi].rearrange("p (n j) -> p n j", j=2), in0=pts[s][:, lo:hi].unsqueeze(2).to_broadcast([P, hi - lo, 2]),
                in1=qts[s][:, 2 * lo : 2 * hi].rearrange("p (n j) -> p n j", j=2), op=ADD)

        def k_store(s, lo=0, hi=1024):
            q, m, half = s // 4, s // 2 % 2, s % 2
            nc.sync.dma_start(out=out_0[q, m * P : (m + 1) * P].rearrange("s h d -> s (h d)")[:, half * 1024 + lo : half * 1024 + hi], in_=oks[s][:, lo:hi])

        vs = {}

        def v_mm(s):
            q, m, half = s // 4, s // 2 % 2, s % 2
            for hh in range(2):
                vs[s, hh] = ps.tile([P, 512], F32, name=f"v{s}_{hh}", tag="v", bufs=2)
                up(q, m, "v", (2 * half + hh) * 512, 512, vs[s, hh][:], True, True)

        def v_out(s):
            q, m, half = s // 4, s // 2 % 2, s % 2
            ov = wk.tile([P, 1024], F32, name=f"ov{s}", tag="ov", bufs=4)
            for hh in range(2):
                nc.scalar.copy(out=ov[:, hh * 512 : (hh + 1) * 512], in_=vs[s, hh][:])
            nc.sync.dma_start(out=out_1[q, m * P : (m + 1) * P].rearrange("s h d -> s (h d)")[:, half * 1024 : (half + 1) * 1024], in_=ov[:])

        cast(0, 0, "s")
        cast(0, 2, "v")
        nc.vector.scalar_tensor_tensor(out=rot[:, :, :, 0], in0=cos[:], scalar=-1.0, in1=sin[:], op0=MULT, op1=SUB)
        nc.vector.scalar_tensor_tensor(out=rot[:, :, :, 1], in0=cos[:], scalar=-1.0, in1=sin[:], op0=MULT, op1=ADD)
        w_lay("c", 0, 0, "v")
        cast(0, 1, "v")
        cast(0, 3, "s")
        w_lay("c", 0, 1, "g")
        nc.vector.tensor_copy(out=gain[:].rearrange("q (u p e) -> q u p e", u=2, e=2), in_=nw[:].rearrange("q (p u e) -> q u p e", u=2, e=2))
        turn(0, 0)
        turn(0, 1)
        w_lay("c", 1, 0, "g")
        w_lay("c", 1, 1, "s")
        prod(0, 0)
        turn(0, 2)
        prod(0, 1)
        turn(0, 3)
        w_lay("c", 2, 0, "g")
        w_lay("c", 2, 1, "s")
        w_lay("c", 3, 0, "g")
        w_lay("c", 3, 1, "s")
        prod(0, 2)
        w_quant("c", 0)
        cast(1, 0, "s")
        cast(1, 1, "s")
        prod(0, 3)
        w_quant("c", 1)
        x_quant(0, 0)
        x_quant(0, 1)
        w_lay("k", 0, 0, "s")
        w_lay("k", 0, 1, "s")
        turn(1, 0)
        w_quant("c", 2)
        w_quant("c", 3)
        compress(0, 0)
        compress(0, 1)
        w_lay("k", 1, 0, "s")
        w_lay("k", 1, 1, "s")
        rms(0, 0)
        rms(0, 1)
        cast(1, 2, "s")
        cast(1, 3, "s")
        prod(1, 0)
        turn(1, 1)
        turn(1, 2)
        norm(0, 0)
        norm(0, 1)
        l_turn(0)
        l_lay(0)
        w_lay("k", 2, 0, "s")
        w_lay("k", 2, 1, "s")
        prod(1, 1)
        w_quant("k", 0)
        w_lay("k", 3, 0, "s")
        w_lay("k", 3, 1, "s")
        prod(1, 2)
        l_quant(0)
        w_quant("k", 1)
        k_b(0)
        x_quant(1, 0)
        w_quant("k", 2)
        turn(1, 3)
        prod(1, 3)
        x_quant(1, 1)
        cast(2, 0, "s")
        cast(2, 1, "s")
        k_a(0)

        extra_lay = {0: [('v', 0, 0, 's'), ('v', 0, 1, 'v'), ('v', 1, 0, 's'), ('v', 1, 1, 'v')], 1: [('v', 2, 0, 's'), ('v', 2, 1, 'v'), ('v', 3, 0, 'g'), ('v', 3, 1, 's')]}
        extra_quant = {1: [('v', 0), ('v', 1), ('v', 2), ('v', 3)]}
        on_s = {10,11,15}
        v_done = 0
        POL = ['gg', 'gg', 'gg', 'vv', 'gg', 'gg', 'gg', 'vv', 'gg', 'gg', 'gg', 'vv', 'gg', 'gg', 'vv', 'vv']
        VT = [0, 0, 0, 2, 4, 6, 8, 8, 12, 12, 12, 12, 16, 16, 16, 16]
        for s in range(16):
            q, i = s // 4, s % 4
            nxt = q + 1 < B
            if s + 10 < 16:
                cast((s + 10) // 4, (s + 10) % 4, "s")
            if q + 2 < B and i % 2 == 0:
                for g in (i, i + 1):
                    turn(q + 2, g)
                    if 4 * q + 8 + g in on_s:
                        prod_s(q + 2, g)
            for item in extra_lay.get(s, []):
                w_lay(*item)
            k_p(s)
            k_q(s, 0)
            k_q(s, 1)
            if s == 0:
                w_quant("k", 3)
            if nxt and i == 3:
                l_quant(q + 1)
            if s + 1 < 16:
                k_b(s + 1)
            if nxt and i in (1, 2):
                norm(q + 1, i - 1)
            if nxt and i < 2:
                compress(q + 1, i)
                rms(q + 1, i)
            if nxt and i == 2:
                l_turn(q + 1)
                l_lay(q + 1)
            for piece, eng in enumerate(POL[s]):
                if eng == "g":
                    k_add(s, "g", piece * 256, (piece + 1) * 256)
            if i % 2 == 0 and q + 2 < B:
                for g in (i, i + 1):
                    if 4 * q + 8 + g not in on_s:
                        prod(q + 2, g)
            for piece, eng in enumerate(POL[s]):
                if eng == "v":
                    k_add(s, "v", piece * 256, (piece + 1) * 256)
            if s == 15:
                k_store(s, 0, 512)
                k_store(s, 512, 1024)
            else:
                k_store(s)
            if i % 2 == 1 and q + 2 < B:
                x_quant(q + 2, i // 2)
            for item in extra_quant.get(s, []):
                w_quant(*item)
            if s + 1 < 16:
                k_a(s + 1)
            target = VT[s]
            while v_done < target:
                v_mm(v_done)
                v_out(v_done)
                v_done += 1
